import numpy as np
import ml_dtypes


def mxq(x, axis, fmt="e4m3"):
    dtype, down = {"e4m3": (ml_dtypes.float8_e4m3fn, 7), "e5m2": (ml_dtypes.float8_e5m2, 14)}[fmt]
    v = np.moveaxis(np.asarray(x, np.float32).astype(ml_dtypes.bfloat16).astype(np.float64), axis, -1)
    blocks = v.reshape(v.shape[:-1] + (-1, 32))
    amax = np.abs(blocks).max(-1, keepdims=True)
    byte = np.maximum(np.where(amax > 0, np.frexp(amax)[1] - 1 + 127, 0) - down, 1)
    scale = np.exp2(byte - 127.0)
    codes = (blocks / scale).astype(np.float32).astype(dtype).astype(np.float64)
    return np.moveaxis((codes * scale).reshape(v.shape), -1, axis)


WIDE = False


def mx_kscale(k):
    if not WIDE:
        return np.ones(k)
    levels = np.array([10, -10, 5, -5, 0])
    a = np.random.permutation(np.resize(levels, k // 512 * 4)).reshape(k // 512, 4)
    idx = np.arange(k)
    return np.exp2(a[idx // 512, idx % 128 // 32])


BF16 = ml_dtypes.bfloat16


def bf(x):
    return np.asarray(x, np.float32).astype(BF16)


def f64(x):
    return np.asarray(x).astype(np.float64)


B, S, H, L, G, NW = 2, 512, 512, 10, 2, 8
OFF = 0.2


def draw(s):
    g = 0.5 + np.random.random_sample((B, S, 1))
    return bf((np.random.standard_normal((B, S, H)) + OFF) * g * s)


def setup_inputs():
    s = mx_kscale(H)
    return {"p": draw(s), "q": draw(1.0 / s)}


def reference(p, q):
    p, q = f64(p), f64(q)
    pn = np.sqrt(np.sum(p * p, axis=2))
    qn = np.sqrt(np.sum(q * q, axis=2))
    dot = mxq(p, 2, "e4m3") @ mxq(q, 2, "e4m3").transpose(0, 2, 1)
    cos = dot / (pn[:, :, None] * qn[:, None, :])
    p_vec = (mxq(cos, 1, "e4m3").transpose(0, 2, 1) @ mxq(p, 1, "e4m3")) / cos.sum(axis=1)[..., None]
    q_vec = (mxq(cos, 2, "e4m3") @ mxq(q, 1, "e4m3")) / cos.sum(axis=2)[..., None]
    return p_vec, q_vec

@@ -1,0 +1,233 @@
+from contextlib import ExitStack
+
+import concourse.mybir as mybir
+from concourse.masks import make_identity
+
+F32 = mybir.dt.float32
+BF16 = mybir.dt.bfloat16
+U32 = mybir.dt.uint32
+U8 = mybir.dt.uint8
+FP8X4 = mybir.dt.float8_e4m3fn_x4
+ACT = mybir.ActivationFunctionType
+ALU = mybir.AluOpType
+
+P = 128
+PACK = 4
+BATCH = 2
+STEPS = 512
+FEATURES = 512
+WIDE = PACK * P * PACK
+
+FLOPS = 3 * 2 * BATCH * STEPS * STEPS * FEATURES
+
+OTHER = {"p": "q", "q": "p"}
+COLUMN = {"p": 0, "q": PACK}
+
+
+def tile_matchinglayer_pb_kernel(tc, p, q, out_0, out_1):
+    nc = tc.nc
+    inputs = {"p": p, "q": q}
+    outputs = {"p": out_0, "q": out_1}
+
+    with ExitStack() as ctx:
+        keep = ctx.enter_context(tc.tile_pool(name="keep", bufs=1))
+        flip_banks = ctx.enter_context(tc.psum_pool(name="flip_banks", bufs=2))
+        sum_banks = ctx.enter_context(tc.psum_pool(name="sum_banks", bufs=6))
+
+        def sbuf(shape, dtype, name):
+            return keep.tile(shape, dtype, name=name, align_bytes=64)
+
+        rows = {}
+        feat_codes, feat_scales = {}, {}
+        step_grouped, step_codes, step_scales = {}, {}, {}
+        square_sums, inv_squares, inv_norms, inv_norm_rows = {}, {}, {}, {}
+        products, cosines, cos_sums, inv_cos_sums = {}, {}, {}, {}
+        cos_codes, cos_scales = {}, {}
+
+        identity = sbuf([P, P], F32, "identity")
+        make_identity(nc, identity[:])
+        one = sbuf([P, 1], F32, "one")
+        nc.vector.memset(one[:], 1.0)
+        warm = sbuf([P, 1], F32, "warm")
+        nc.scalar.activation(out=warm[:], in_=one[:], func=ACT.Sqrt)
+
+        def load(b, m):
+            rows[m, b] = sbuf([P, WIDE], BF16, "rows_%s%d" % (m, b))
+            nc.sync.dma_start(
+                out=rows[m, b][:],
+                in_=inputs[m][b].rearrange("(r t) h -> r (t h)", t=PACK),
+            )
+
+        def regroup(dst, src):
+            nc.vector.tensor_copy(
+                out=dst[:].rearrange("p (c i t) -> p c t i", i=4, t=PACK),
+                in_=src[:].rearrange("p (t c i) -> p c t i", i=4, t=PACK),
+            )
+
+        def quantise(grouped, name):
+            codes = sbuf([P, WIDE // PACK], U32, "codes_" + name)
+            scales = sbuf([P, WIDE // PACK], U8, "scales_" + name)
+            nc.vector.quantize_mx(out=codes[:].bitcast(FP8X4), scales=scales[:], in_=grouped[:])
+            return codes, scales
+
+        feat_grouped = {}
+
+        def flip_features(b, m, copy):
+            words = rows[m, b][:].bitcast(F32)
+            grouped = sbuf([P, WIDE], BF16, "feat_grouped_%s%d" % (m, b))
+            feat_grouped[m, b] = grouped
+            grouped_words = grouped[:].bitcast(F32).rearrange(
+                "p (g t r u) -> p g t r u", g=2, t=2, u=2
+            )
+            for g in range(2):
+                bank = flip_banks.tile([P, 2, 2, P], F32, name="flipped", tag="flip")
+                for t in range(2):
+                    for u in range(2):
+                        first = (2 * g + t) * (FEATURES // 2) + u * P
+                        nc.tensor.transpose(bank[:, t, u, :], words[:, first : first + P], identity[:])
+                copy(out=grouped_words[:, g], in_=bank[:].rearrange("p t u r -> p t r u"))
+
+        def quantise_features(b, m):
+            feat_codes[m, b], feat_scales[m, b] = quantise(feat_grouped[m, b], "feat_%s%d" % (m, b))
+
+        def sum_squares(b, m):
+            if b not in square_sums:
+                square_sums[b] = sbuf([P, 2 * PACK], F32, "square_sums%d" % b)
+            squares = sbuf([P, WIDE], BF16, "squares_%s%d" % (m, b))
+            for t in range(PACK):
+                cols = slice(t * FEATURES, (t + 1) * FEATURES)
+                nc.scalar.activation(
+                    out=squares[:, cols],
+                    in_=rows[m, b][:, cols],
+                    func=ACT.Square,
+                    accum_out=square_sums[b][:, COLUMN[m] + t : COLUMN[m] + t + 1],
+                )
+
+        def regroup_steps(b, m):
+            step_grouped[m, b] = sbuf([P, WIDE], BF16, "step_grouped_%s%d" % (m, b))
+            regroup(step_grouped[m, b], rows[m, b])
+
+        def quantise_steps(b, m):
+            step_codes[m, b], step_scales[m, b] = quantise(step_grouped[m, b], "step_%s%d" % (m, b))
+
+        def invert_norms(b):
+            inv_squares[b] = sbuf([P, 2 * PACK], F32, "inv_squares%d" % b)
+            nc.vector.reciprocal(out=inv_squares[b][:], in_=square_sums[b][:])
+            inv_norms[b] = sbuf([P, 2 * PACK, P], F32, "inv_norms%d" % b)
+            nc.scalar.activation(
+                out=inv_norms[b][:],
+                in_=inv_squares[b][:].unsqueeze(2).to_broadcast([P, 2 * PACK, P]),
+                func=ACT.Sqrt,
+            )
+            for m in ("q", "p"):
+                bank = flip_banks.tile([P, PACK, P], F32, name="norm_rows", tag="flip")
+                for t in range(PACK):
+                    nc.tensor.transpose(bank[:, t, :], inv_norms[b][:, COLUMN[m] + t, :], identity[:])
+                inv_norm_rows[m, b] = sbuf([P, STEPS], F32, "inv_norm_rows_%s%d" % (m, b))
+                nc.scalar.copy(out=inv_norm_rows[m, b][:], in_=bank[:].rearrange("p t r -> p (t r)"))
+
+        def product(b, m, t):
+            o = OTHER[m]
+            tile_cols = slice(t * P, (t + 1) * P)
+            bank = sum_banks.tile([P, STEPS], F32, name="product", tag="sum")
+            nc.tensor.matmul_mx(
+                out=bank[:],
+                lhsT=feat_codes[m, b][:, tile_cols].bitcast(FP8X4),
+                lhsT_scale=feat_scales[m, b][:, tile_cols],
+                rhs=feat_codes[o, b][:].bitcast(FP8X4),
+                rhs_scale=feat_scales[o, b][:],
+                start=True,
+                stop=True,
+            )
+            products[m, b, t] = bank
+
+        def normalise(b, m, t):
+            if b not in cos_sums:
+                cos_sums[b] = sbuf([P, 2 * PACK], F32, "cos_sums%d" % b)
+            if (m, b) not in cosines:
+                cosines[m, b] = sbuf([P, WIDE], BF16, "cosines_%s%d" % (m, b))
+            nc.vector.scalar_tensor_tensor(
+                out=cosines[m, b][:, t * STEPS : (t + 1) * STEPS],
+                in0=products[m, b, t][:],
+                scalar=inv_norms[b][:, COLUMN[m] + t, 0:1],
+                in1=inv_norm_rows[OTHER[m], b][:],
+                op0=ALU.mult,
+                op1=ALU.mult,
+                accum_out=cos_sums[b][:, COLUMN[m] + t : COLUMN[m] + t + 1],
+            )
+
+        def pack_cosines(b):
+            inv_cos_sums[b] = sbuf([P, 2 * PACK], F32, "inv_cos_sums%d" % b)
+            nc.vector.reciprocal(out=inv_cos_sums[b][:], in_=cos_sums[b][:])
+            grouped = {}
+            for m in ("p", "q"):
+                grouped[m] = sbuf([P, WIDE], BF16, "cos_grouped_%s%d" % (m, b))
+                regroup(grouped[m], cosines[m, b])
+            for m in ("p", "q"):
+                cos_codes[m, b], cos_scales[m, b] = quantise(grouped[m], "cos_%s%d" % (m, b))
+
+        def vectors(b, m):
+            o = OTHER[m]
+            result = sbuf([P, PACK, FEATURES], F32, "result_%s%d" % (m, b))
+            out_rows = outputs[m][b].rearrange("(r t) h -> r t h", t=PACK)
+            for t in range(PACK):
+                tile_cols = slice(t * P, (t + 1) * P)
+                bank = sum_banks.tile([P, FEATURES], F32, name="weighted", tag="sum")
+                nc.tensor.matmul_mx(
+                    out=bank[:],
+                    lhsT=cos_codes[m, b][:, tile_cols].bitcast(FP8X4),
+                    lhsT_scale=cos_scales[m, b][:, tile_cols],
+                    rhs=step_codes[m, b][:].bitcast(FP8X4),
+                    rhs_scale=step_scales[m, b][:],
+                    start=True,
+                    stop=True,
+                )
+                inv_sum = inv_cos_sums[b][:, COLUMN[o] + t : COLUMN[o] + t + 1]
+                if b == BATCH - 1 and t % 2 == 1:
+                    nc.vector.tensor_scalar_mul(out=result[:, t, :], in0=bank[:], scalar1=inv_sum)
+                else:
+                    nc.scalar.activation(out=result[:, t, :], in_=bank[:], func=ACT.Copy, scale=inv_sum)
+                nc.sync.dma_start(out=out_rows[:, t, :], in_=result[:, t, :])
+
+        ctx.enter_context(tc.manual_schedule())
+
+        for b in range(BATCH):
+            for m in ("p", "q"):
+                load(b, m)
+
+        for m in ("p", "q"):
+            flip_features(0, m, nc.vector.tensor_copy)
+            sum_squares(0, m)
+            regroup_steps(0, m)
+        for m in ("p", "q"):
+            quantise_features(0, m)
+        invert_norms(0)
+        for m in ("p", "q"):
+            quantise_steps(0, m)
+
+        for b in range(BATCH):
+            for t in range(PACK):
+                product(b, "p", t)
+            if b + 1 < BATCH:
+                for m in ("p", "q"):
+                    flip_features(b + 1, m, nc.scalar.copy)
+                    sum_squares(b + 1, m)
+                    regroup_steps(b + 1, m)
+                for m in ("p", "q"):
+                    quantise_steps(b + 1, m)
+            if b > 0:
+                vectors(b - 1, "p")
+            for t in range(PACK):
+                normalise(b, "p", t)
+                product(b, "q", t)
+            if b > 0:
+                vectors(b - 1, "q")
+            for t in range(PACK):
+                normalise(b, "q", t)
+            if b + 1 < BATCH:
+                invert_norms(b + 1)
+                for m in ("p", "q"):
+                    quantise_features(b + 1, m)
+            pack_cosines(b)
+        vectors(BATCH - 1, "p")
+        vectors(BATCH - 1, "q")

@@ -14,14 +14,15 @@ ALU = mybir.AluOpType
 P = 128
 PACK = 4
 BATCH = 2
-STEPS = 512
-FEATURES = 512
-WIDE = PACK * P * PACK
+STEPS = P * PACK
+FEATURES = P * PACK
+MATRIX = PACK * FEATURES
 
 FLOPS = 3 * 2 * BATCH * STEPS * STEPS * FEATURES
 
+SIDES = ("p", "q")
 OTHER = {"p": "q", "q": "p"}
-COLUMN = {"p": 0, "q": PACK}
+FIRST = {"p": 0, "q": PACK}
 
 
 def tile_matchinglayer_pb_kernel(tc, p, q, out_0, out_1):
@@ -32,17 +33,176 @@ def tile_matchinglayer_pb_kernel(tc, p, q, out_0, out_1):
     with ExitStack() as ctx:
         keep = ctx.enter_context(tc.tile_pool(name="keep", bufs=1))
         flip_banks = ctx.enter_context(tc.psum_pool(name="flip_banks", bufs=2))
-        sum_banks = ctx.enter_context(tc.psum_pool(name="sum_banks", bufs=6))
+        product_banks = ctx.enter_context(tc.psum_pool(name="product_banks", bufs=PACK))
+        weighted_banks = ctx.enter_context(tc.psum_pool(name="weighted_banks", bufs=2))
 
         def sbuf(shape, dtype, name):
             return keep.tile(shape, dtype, name=name, align_bytes=64)
 
         rows = {}
-        feat_codes, feat_scales = {}, {}
+        feature_grouped, feature_codes, feature_scales = {}, {}, {}
         step_grouped, step_codes, step_scales = {}, {}, {}
-        square_sums, inv_squares, inv_norms, inv_norm_rows = {}, {}, {}, {}
-        products, cosines, cos_sums, inv_cos_sums = {}, {}, {}, {}
-        cos_codes, cos_scales = {}, {}
+        square_sums, inv_norms, inv_norm_rows = {}, {}, {}
+        products, cosines, cos_grouped, cos_codes, cos_scales = {}, {}, {}, {}, {}
+        cos_sums, inv_cos_sums = {}, {}
+
+        def load(b, m):
+            rows[m, b] = sbuf([P, MATRIX], BF16, "rows_%s%d" % (m, b))
+            nc.sync.dma_start(
+                out=rows[m, b][:],
+                in_=inputs[m][b].rearrange("(r t) h -> r (t h)", t=PACK),
+            )
+
+
+        def regroup(engine, dst, src):
+            if engine == "gpsimd":
+                nc.gpsimd.tensor_scalar(
+                    out=dst[:].rearrange("r (c t) -> r c t", t=PACK),
+                    in0=src[:].rearrange("r (t c) -> r c t", t=PACK),
+                    scalar1=1.0,
+                    scalar2=0.0,
+                    op0=ALU.mult,
+                    op1=ALU.add,
+                )
+            else:
+                copy = nc.vector.tensor_copy if engine == "vector" else nc.scalar.copy
+                copy(
+                    out=dst[:].rearrange("r (c i t) -> r c t i", i=4, t=PACK),
+                    in_=src[:].rearrange("r (t c i) -> r c t i", i=4, t=PACK),
+                )
+
+        def quantise(grouped, name):
+            codes = sbuf([P, MATRIX // PACK], U32, "codes_" + name)
+            scales = sbuf([P, MATRIX // PACK], U8, "scales_" + name)
+            nc.vector.quantize_mx(out=codes[:].bitcast(FP8X4), scales=scales[:], in_=grouped[:])
+            return codes, scales
+
+        def flip_features(b, m):
+            words = rows[m, b][:].bitcast(F32)
+            grouped = sbuf([P, MATRIX], BF16, "feature_grouped_%s%d" % (m, b))
+            feature_grouped[m, b] = grouped
+            grouped_words = grouped[:].bitcast(F32).rearrange("w (g t r u) -> w g t r u", g=2, t=2, u=2)
+            for g in range(2):
+                bank = flip_banks.tile([P, 2, 2, P], F32, name="flipped", tag="flip")
+                for t in range(2):
+                    for u in range(2):
+                        first = (2 * g + t) * (FEATURES // 2) + u * P
+                        nc.tensor.transpose(bank[:, t, u, :], words[:, first : first + P], identity[:])
+                nc.vector.tensor_copy(out=grouped_words[:, g], in_=bank[:].rearrange("w t u r -> w t r u"))
+
+        def quantise_features(b, m):
+            feature_codes[m, b], feature_scales[m, b] = quantise(
+                feature_grouped[m, b], "feature_%s%d" % (m, b)
+            )
+
+        def regroup_steps(engine, b, m):
+            step_grouped[m, b] = sbuf([P, MATRIX], BF16, "step_grouped_%s%d" % (m, b))
+            regroup(engine, step_grouped[m, b], rows[m, b])
+
+        def quantise_steps(b, m):
+            step_codes[m, b], step_scales[m, b] = quantise(step_grouped[m, b], "step_%s%d" % (m, b))
+
+
+        def sum_squares(b, m):
+            if b not in square_sums:
+                square_sums[b] = sbuf([P, 2 * PACK], F32, "square_sums%d" % b)
+            squares = sbuf([P, MATRIX], BF16, "squares_%s%d" % (m, b))
+            for t in range(PACK):
+                cols = slice(t * FEATURES, (t + 1) * FEATURES)
+                nc.scalar.activation(
+                    out=squares[:, cols],
+                    in_=rows[m, b][:, cols],
+                    func=ACT.Square,
+                    accum_out=square_sums[b][:, FIRST[m] + t : FIRST[m] + t + 1],
+                )
+
+        def invert_norms(b):
+            inv_squares = sbuf([P, 2 * PACK], F32, "inv_squares%d" % b)
+            nc.vector.reciprocal(out=inv_squares[:], in_=square_sums[b][:])
+            inv_norms[b] = sbuf([P, 2 * PACK], F32, "inv_norms%d" % b)
+            nc.scalar.activation(out=inv_norms[b][:], in_=inv_squares[:], func=ACT.Sqrt)
+
+        def spread_inv_norms(b, m):
+            bank = flip_banks.tile([P, PACK, P], F32, name="spread", tag="flip")
+            for t in range(PACK):
+                column = inv_norms[b][:, FIRST[m] + t : FIRST[m] + t + 1]
+                nc.tensor.matmul(
+                    out=bank[:, t, :], lhsT=column.to_broadcast([P, P]), rhs=identity[:], start=True, stop=True
+                )
+            inv_norm_rows[m, b] = sbuf([P, STEPS], F32, "inv_norm_rows_%s%d" % (m, b))
+            nc.scalar.copy(out=inv_norm_rows[m, b][:], in_=bank[:].rearrange("k t r -> k (t r)"))
+
+
+        def multiply_features(b, m):
+            o = OTHER[m]
+            for t in range(PACK):
+                tile_cols = slice(t * P, (t + 1) * P)
+                products[m, b, t] = product_banks.tile([P, STEPS], F32, name="product", tag="product")
+                nc.tensor.matmul_mx(
+                    out=products[m, b, t][:],
+                    lhsT=feature_codes[m, b][:, tile_cols].bitcast(FP8X4),
+                    lhsT_scale=feature_scales[m, b][:, tile_cols],
+                    rhs=feature_codes[o, b][:].bitcast(FP8X4),
+                    rhs_scale=feature_scales[o, b][:],
+                    start=True,
+                    stop=True,
+                )
+
+        def normalise(b, m, t):
+            if b not in cos_sums:
+                cos_sums[b] = sbuf([P, 2 * PACK], F32, "cos_sums%d" % b)
+            if (m, b) not in cosines:
+                cosines[m, b] = sbuf([P, MATRIX], BF16, "cosines_%s%d" % (m, b))
+            nc.vector.scalar_tensor_tensor(
+                out=cosines[m, b][:, t * STEPS : (t + 1) * STEPS],
+                in0=products[m, b, t][:],
+                scalar=inv_norms[b][:, FIRST[m] + t : FIRST[m] + t + 1],
+                in1=inv_norm_rows[OTHER[m], b][:],
+                op0=ALU.mult,
+                op1=ALU.mult,
+                accum_out=cos_sums[b][:, FIRST[m] + t : FIRST[m] + t + 1],
+            )
+
+        def regroup_cosines(engine, b, m):
+            cos_grouped[m, b] = sbuf([P, MATRIX], BF16, "cos_grouped_%s%d" % (m, b))
+            regroup(engine, cos_grouped[m, b], cosines[m, b])
+
+        def quantise_cosines(b, m):
+            cos_codes[m, b], cos_scales[m, b] = quantise(cos_grouped[m, b], "cos_%s%d" % (m, b))
+
+        def invert_cos_sums(b):
+            inv_cos_sums[b] = sbuf([P, 2 * PACK], F32, "inv_cos_sums%d" % b)
+            nc.vector.reciprocal(out=inv_cos_sums[b][:], in_=cos_sums[b][:])
+
+
+        results = {}
+        banks = {"weighted": weighted_banks, "product": product_banks}
+
+        def mean_vectors(b, m, t, kind, engine):
+            o = OTHER[m]
+            if (m, b) not in results:
+                results[m, b] = sbuf([P, PACK, FEATURES], F32, "result_%s%d" % (m, b))
+            tile_cols = slice(t * P, (t + 1) * P)
+            bank = banks[kind].tile([P, FEATURES], F32, name="weighted_sum", tag=kind)
+            nc.tensor.matmul_mx(
+                out=bank[:],
+                lhsT=cos_codes[m, b][:, tile_cols].bitcast(FP8X4),
+                lhsT_scale=cos_scales[m, b][:, tile_cols],
+                rhs=step_codes[m, b][:].bitcast(FP8X4),
+                rhs_scale=step_scales[m, b][:],
+                start=True,
+                stop=True,
+            )
+            inv_sum = inv_cos_sums[b][:, FIRST[o] + t : FIRST[o] + t + 1]
+            if engine == "vector":
+                nc.vector.tensor_scalar_mul(out=results[m, b][:, t, :], in0=bank[:], scalar1=inv_sum)
+            else:
+                nc.scalar.activation(out=results[m, b][:, t, :], in_=bank[:], func=ACT.Copy, scale=inv_sum)
+            nc.sync.dma_start(
+                out=outputs[m][b].rearrange("(r t) h -> r t h", t=PACK)[:, t, :], in_=results[m, b][:, t, :]
+            )
+
+        ctx.enter_context(tc.manual_schedule())
 
         identity = sbuf([P, P], F32, "identity")
         make_identity(nc, identity[:])
@@ -51,183 +211,63 @@ def tile_matchinglayer_pb_kernel(tc, p, q, out_0, out_1):
         warm = sbuf([P, 1], F32, "warm")
         nc.scalar.activation(out=warm[:], in_=one[:], func=ACT.Sqrt)
 
-        def load(b, m):
-            rows[m, b] = sbuf([P, WIDE], BF16, "rows_%s%d" % (m, b))
-            nc.sync.dma_start(
-                out=rows[m, b][:],
-                in_=inputs[m][b].rearrange("(r t) h -> r (t h)", t=PACK),
-            )
-
-        def regroup(dst, src):
-            nc.vector.tensor_copy(
-                out=dst[:].rearrange("p (c i t) -> p c t i", i=4, t=PACK),
-                in_=src[:].rearrange("p (t c i) -> p c t i", i=4, t=PACK),
-            )
-
-        def quantise(grouped, name):
-            codes = sbuf([P, WIDE // PACK], U32, "codes_" + name)
-            scales = sbuf([P, WIDE // PACK], U8, "scales_" + name)
-            nc.vector.quantize_mx(out=codes[:].bitcast(FP8X4), scales=scales[:], in_=grouped[:])
-            return codes, scales
-
-        feat_grouped = {}
-
-        def flip_features(b, m, copy):
-            words = rows[m, b][:].bitcast(F32)
-            grouped = sbuf([P, WIDE], BF16, "feat_grouped_%s%d" % (m, b))
-            feat_grouped[m, b] = grouped
-            grouped_words = grouped[:].bitcast(F32).rearrange(
-                "p (g t r u) -> p g t r u", g=2, t=2, u=2
-            )
-            for g in range(2):
-                bank = flip_banks.tile([P, 2, 2, P], F32, name="flipped", tag="flip")
-                for t in range(2):
-                    for u in range(2):
-                        first = (2 * g + t) * (FEATURES // 2) + u * P
-                        nc.tensor.transpose(bank[:, t, u, :], words[:, first : first + P], identity[:])
-                copy(out=grouped_words[:, g], in_=bank[:].rearrange("p t u r -> p t r u"))
-
-        def quantise_features(b, m):
-            feat_codes[m, b], feat_scales[m, b] = quantise(feat_grouped[m, b], "feat_%s%d" % (m, b))
-
-        def sum_squares(b, m):
-            if b not in square_sums:
-                square_sums[b] = sbuf([P, 2 * PACK], F32, "square_sums%d" % b)
-            squares = sbuf([P, WIDE], BF16, "squares_%s%d" % (m, b))
-            for t in range(PACK):
-                cols = slice(t * FEATURES, (t + 1) * FEATURES)
-                nc.scalar.activation(
-                    out=squares[:, cols],
-                    in_=rows[m, b][:, cols],
-                    func=ACT.Square,
-                    accum_out=square_sums[b][:, COLUMN[m] + t : COLUMN[m] + t + 1],
-                )
-
-        def regroup_steps(b, m):
-            step_grouped[m, b] = sbuf([P, WIDE], BF16, "step_grouped_%s%d" % (m, b))
-            regroup(step_grouped[m, b], rows[m, b])
-
-        def quantise_steps(b, m):
-            step_codes[m, b], step_scales[m, b] = quantise(step_grouped[m, b], "step_%s%d" % (m, b))
-
-        def invert_norms(b):
-            inv_squares[b] = sbuf([P, 2 * PACK], F32, "inv_squares%d" % b)
-            nc.vector.reciprocal(out=inv_squares[b][:], in_=square_sums[b][:])
-            inv_norms[b] = sbuf([P, 2 * PACK, P], F32, "inv_norms%d" % b)
-            nc.scalar.activation(
-                out=inv_norms[b][:],
-                in_=inv_squares[b][:].unsqueeze(2).to_broadcast([P, 2 * PACK, P]),
-                func=ACT.Sqrt,
-            )
-            for m in ("q", "p"):
-                bank = flip_banks.tile([P, PACK, P], F32, name="norm_rows", tag="flip")
-                for t in range(PACK):
-                    nc.tensor.transpose(bank[:, t, :], inv_norms[b][:, COLUMN[m] + t, :], identity[:])
-                inv_norm_rows[m, b] = sbuf([P, STEPS], F32, "inv_norm_rows_%s%d" % (m, b))
-                nc.scalar.copy(out=inv_norm_rows[m, b][:], in_=bank[:].rearrange("p t r -> p (t r)"))
-
-        def product(b, m, t):
-            o = OTHER[m]
-            tile_cols = slice(t * P, (t + 1) * P)
-            bank = sum_banks.tile([P, STEPS], F32, name="product", tag="sum")
-            nc.tensor.matmul_mx(
-                out=bank[:],
-                lhsT=feat_codes[m, b][:, tile_cols].bitcast(FP8X4),
-                lhsT_scale=feat_scales[m, b][:, tile_cols],
-                rhs=feat_codes[o, b][:].bitcast(FP8X4),
-                rhs_scale=feat_scales[o, b][:],
-                start=True,
-                stop=True,
-            )
-            products[m, b, t] = bank
-
-        def normalise(b, m, t):
-            if b not in cos_sums:
-                cos_sums[b] = sbuf([P, 2 * PACK], F32, "cos_sums%d" % b)
-            if (m, b) not in cosines:
-                cosines[m, b] = sbuf([P, WIDE], BF16, "cosines_%s%d" % (m, b))
-            nc.vector.scalar_tensor_tensor(
-                out=cosines[m, b][:, t * STEPS : (t + 1) * STEPS],
-                in0=products[m, b, t][:],
-                scalar=inv_norms[b][:, COLUMN[m] + t, 0:1],
-                in1=inv_norm_rows[OTHER[m], b][:],
-                op0=ALU.mult,
-                op1=ALU.mult,
-                accum_out=cos_sums[b][:, COLUMN[m] + t : COLUMN[m] + t + 1],
-            )
-
-        def pack_cosines(b):
-            inv_cos_sums[b] = sbuf([P, 2 * PACK], F32, "inv_cos_sums%d" % b)
-            nc.vector.reciprocal(out=inv_cos_sums[b][:], in_=cos_sums[b][:])
-            grouped = {}
-            for m in ("p", "q"):
-                grouped[m] = sbuf([P, WIDE], BF16, "cos_grouped_%s%d" % (m, b))
-                regroup(grouped[m], cosines[m, b])
-            for m in ("p", "q"):
-                cos_codes[m, b], cos_scales[m, b] = quantise(grouped[m], "cos_%s%d" % (m, b))
-
-        def vectors(b, m):
-            o = OTHER[m]
-            result = sbuf([P, PACK, FEATURES], F32, "result_%s%d" % (m, b))
-            out_rows = outputs[m][b].rearrange("(r t) h -> r t h", t=PACK)
-            for t in range(PACK):
-                tile_cols = slice(t * P, (t + 1) * P)
-                bank = sum_banks.tile([P, FEATURES], F32, name="weighted", tag="sum")
-                nc.tensor.matmul_mx(
-                    out=bank[:],
-                    lhsT=cos_codes[m, b][:, tile_cols].bitcast(FP8X4),
-                    lhsT_scale=cos_scales[m, b][:, tile_cols],
-                    rhs=step_codes[m, b][:].bitcast(FP8X4),
-                    rhs_scale=step_scales[m, b][:],
-                    start=True,
-                    stop=True,
-                )
-                inv_sum = inv_cos_sums[b][:, COLUMN[o] + t : COLUMN[o] + t + 1]
-                if b == BATCH - 1 and t % 2 == 1:
-                    nc.vector.tensor_scalar_mul(out=result[:, t, :], in0=bank[:], scalar1=inv_sum)
-                else:
-                    nc.scalar.activation(out=result[:, t, :], in_=bank[:], func=ACT.Copy, scale=inv_sum)
-                nc.sync.dma_start(out=out_rows[:, t, :], in_=result[:, t, :])
-
-        ctx.enter_context(tc.manual_schedule())
-
         for b in range(BATCH):
-            for m in ("p", "q"):
+            for m in SIDES:
                 load(b, m)
 
-        for m in ("p", "q"):
-            flip_features(0, m, nc.vector.tensor_copy)
+        for m in SIDES:
+            regroup_steps("gpsimd", 0, m)
             sum_squares(0, m)
-            regroup_steps(0, m)
-        for m in ("p", "q"):
-            quantise_features(0, m)
+        for b in range(BATCH):
+            for m in SIDES:
+                flip_features(b, m)
         invert_norms(0)
-        for m in ("p", "q"):
+        sum_squares(1, "p")
+        spread_inv_norms(0, "q")
+        spread_inv_norms(0, "p")
+        sum_squares(1, "q")
+        for b in range(BATCH):
+            for m in SIDES:
+                quantise_features(b, m)
+        multiply_features(0, "p")
+        for m in SIDES:
             quantise_steps(0, m)
 
-        for b in range(BATCH):
-            for t in range(PACK):
-                product(b, "p", t)
-            if b + 1 < BATCH:
-                for m in ("p", "q"):
-                    flip_features(b + 1, m, nc.scalar.copy)
-                    sum_squares(b + 1, m)
-                    regroup_steps(b + 1, m)
-                for m in ("p", "q"):
-                    quantise_steps(b + 1, m)
-            if b > 0:
-                vectors(b - 1, "p")
-            for t in range(PACK):
-                normalise(b, "p", t)
-                product(b, "q", t)
-            if b > 0:
-                vectors(b - 1, "q")
-            for t in range(PACK):
-                normalise(b, "q", t)
-            if b + 1 < BATCH:
-                invert_norms(b + 1)
-                for m in ("p", "q"):
-                    quantise_features(b + 1, m)
-            pack_cosines(b)
-        vectors(BATCH - 1, "p")
-        vectors(BATCH - 1, "q")
+        for t in range(PACK):
+            normalise(0, "p", t)
+        regroup_cosines("gpsimd", 0, "p")
+        multiply_features(0, "q")
+        regroup_steps("vector", 1, "p")
+        invert_norms(1)
+        regroup_steps("scalar", 1, "q")
+        spread_inv_norms(1, "q")
+        spread_inv_norms(1, "p")
+
+        for t in range(PACK):
+            normalise(0, "q", t)
+        invert_cos_sums(0)
+        regroup_cosines("gpsimd", 0, "q")
+        multiply_features(1, "p")
+        quantise_steps(1, "p")
+        quantise_cosines(0, "p")
+
+        for t in range(PACK):
+            normalise(1, "p", t)
+            mean_vectors(0, "p", t, "weighted", "scalar")
+        regroup_cosines("gpsimd", 1, "p")
+        multiply_features(1, "q")
+        quantise_steps(1, "q")
+        quantise_cosines(0, "q")
+
+        for t in range(PACK):
+            normalise(1, "q", t)
+            mean_vectors(0, "q", t, "weighted", "scalar")
+        invert_cos_sums(1)
+        quantise_cosines(1, "p")
+        regroup_cosines("vector", 1, "q")
+
+        for t in range(PACK):
+            mean_vectors(1, "p", t, ("weighted", "product")[t % 2], "scalar")
+        quantise_cosines(1, "q")
+        for t in range(PACK):
+            mean_vectors(1, "q", t, ("weighted", "product")[t % 2], ("vector", "scalar")[t % 2])

@@ -202,8 +202,6 @@ def tile_matchinglayer_pb_kernel(tc, p, q, out_0, out_1):
                 out=outputs[m][b].rearrange("(r t) h -> r t h", t=PACK)[:, t, :], in_=results[m, b][:, t, :]
             )
 
-        ctx.enter_context(tc.manual_schedule())
-
         identity = sbuf([P, P], F32, "identity")
         make_identity(nc, identity[:])
         one = sbuf([P, 1], F32, "one")

@@ -46,12 +46,13 @@ def tile_matchinglayer_pb_kernel(tc, p, q, out_0, out_1):
         products, cosines, cos_grouped, cos_codes, cos_scales = {}, {}, {}, {}, {}
         cos_sums, inv_cos_sums = {}, {}
 
-        def load(b, m):
+        def load(b, m, pieces):
             rows[m, b] = sbuf([P, MATRIX], BF16, "rows_%s%d" % (m, b))
-            nc.sync.dma_start(
-                out=rows[m, b][:],
-                in_=inputs[m][b].rearrange("(r t) h -> r (t h)", t=PACK),
-            )
+            source = inputs[m][b].rearrange("(r t) h -> r (t h)", t=PACK)
+            width = MATRIX // pieces
+            for i in range(pieces):
+                cols = slice(i * width, (i + 1) * width)
+                nc.sync.dma_start(out=rows[m, b][:, cols], in_=source[:, cols])
 
 
         def regroup(engine, dst, src):
@@ -202,6 +203,8 @@ def tile_matchinglayer_pb_kernel(tc, p, q, out_0, out_1):
                 out=outputs[m][b].rearrange("(r t) h -> r t h", t=PACK)[:, t, :], in_=results[m, b][:, t, :]
             )
 
+        ctx.enter_context(tc.manual_schedule())
+
         identity = sbuf([P, P], F32, "identity")
         make_identity(nc, identity[:])
         one = sbuf([P, 1], F32, "one")
@@ -211,7 +214,7 @@ def tile_matchinglayer_pb_kernel(tc, p, q, out_0, out_1):
 
         for b in range(BATCH):
             for m in SIDES:
-                load(b, m)
+                load(b, m, pieces=2 if b == 0 else 1)
 
         for m in SIDES:
             regroup_steps("gpsimd", 0, m)
@@ -220,14 +223,14 @@ def tile_matchinglayer_pb_kernel(tc, p, q, out_0, out_1):
             for m in SIDES:
                 flip_features(b, m)
         invert_norms(0)
-        sum_squares(1, "p")
-        spread_inv_norms(0, "q")
-        spread_inv_norms(0, "p")
-        sum_squares(1, "q")
         for b in range(BATCH):
             for m in SIDES:
                 quantise_features(b, m)
+        sum_squares(1, "p")
+        spread_inv_norms(0, "q")
         multiply_features(0, "p")
+        sum_squares(1, "q")
+        spread_inv_norms(0, "p")
         for m in SIDES:
             quantise_steps(0, m)
 
@@ -239,13 +242,13 @@ def tile_matchinglayer_pb_kernel(tc, p, q, out_0, out_1):
         invert_norms(1)
         regroup_steps("scalar", 1, "q")
         spread_inv_norms(1, "q")
-        spread_inv_norms(1, "p")
 
         for t in range(PACK):
             normalise(0, "q", t)
         invert_cos_sums(0)
         regroup_cosines("gpsimd", 0, "q")
         multiply_features(1, "p")
+        spread_inv_norms(1, "p")
         quantise_steps(1, "p")
         quantise_cosines(0, "p")
 

@@ -35,6 +35,7 @@ def tile_matchinglayer_pb_kernel(tc, p, q, out_0, out_1):
         flip_banks = ctx.enter_context(tc.psum_pool(name="flip_banks", bufs=2))
         product_banks = ctx.enter_context(tc.psum_pool(name="product_banks", bufs=PACK))
         weighted_banks = ctx.enter_context(tc.psum_pool(name="weighted_banks", bufs=2))
+        banks = {"flip": flip_banks, "product": product_banks, "weighted": weighted_banks}
 
         def sbuf(shape, dtype, name):
             return keep.tile(shape, dtype, name=name, align_bytes=64)
@@ -84,7 +85,8 @@ def tile_matchinglayer_pb_kernel(tc, p, q, out_0, out_1):
             feature_grouped[m, b] = grouped
             grouped_words = grouped[:].bitcast(F32).rearrange("w (g t r u) -> w g t r u", g=2, t=2, u=2)
             for g in range(2):
-                bank = flip_banks.tile([P, 2, 2, P], F32, name="flipped", tag="flip")
+                kind = ("flip", "weighted")[g]
+                bank = banks[kind].tile([P, 2, 2, P], F32, name="flipped", tag=kind)
                 for t in range(2):
                     for u in range(2):
                         first = (2 * g + t) * (FEATURES // 2) + u * P
@@ -177,7 +179,6 @@ def tile_matchinglayer_pb_kernel(tc, p, q, out_0, out_1):
 
 
         results = {}
-        banks = {"weighted": weighted_banks, "product": product_banks}
 
         def mean_vectors(b, m, t, kind, engine):
             o = OTHER[m]
@@ -238,7 +239,6 @@ def tile_matchinglayer_pb_kernel(tc, p, q, out_0, out_1):
             normalise(0, "p", t)
         regroup_cosines("gpsimd", 0, "p")
         multiply_features(0, "q")
-        regroup_steps("vector", 1, "p")
         invert_norms(1)
         regroup_steps("scalar", 1, "q")
         spread_inv_norms(1, "q")
@@ -248,8 +248,9 @@ def tile_matchinglayer_pb_kernel(tc, p, q, out_0, out_1):
         invert_cos_sums(0)
         regroup_cosines("gpsimd", 0, "q")
         multiply_features(1, "p")
+        regroup_steps("scalar", 1, "p")
         spread_inv_norms(1, "p")
-        quantise_steps(1, "p")
+        quantise_steps(1, "q")
         quantise_cosines(0, "p")
 
         for t in range(PACK):
@@ -257,7 +258,7 @@ def tile_matchinglayer_pb_kernel(tc, p, q, out_0, out_1):
             mean_vectors(0, "p", t, "weighted", "scalar")
         regroup_cosines("gpsimd", 1, "p")
         multiply_features(1, "q")
-        quantise_steps(1, "q")
+        quantise_steps(1, "p")
         quantise_cosines(0, "q")
 
         for t in range(PACK):

from contextlib import ExitStack

import concourse.mybir as mybir
from concourse.masks import make_identity

F32 = mybir.dt.float32
BF16 = mybir.dt.bfloat16
U32 = mybir.dt.uint32
U8 = mybir.dt.uint8
FP8X4 = mybir.dt.float8_e4m3fn_x4
ACT = mybir.ActivationFunctionType
ALU = mybir.AluOpType

P = 128
PACK = 4
BATCH = 2
STEPS = P * PACK
FEATURES = P * PACK
MATRIX = PACK * FEATURES

FLOPS = 3 * 2 * BATCH * STEPS * STEPS * FEATURES

SIDES = ("p", "q")
OTHER = {"p": "q", "q": "p"}
FIRST = {"p": 0, "q": PACK}


def tile_matchinglayer_pb_kernel(tc, p, q, out_0, out_1):
    nc = tc.nc
    inputs = {"p": p, "q": q}
    outputs = {"p": out_0, "q": out_1}

    with ExitStack() as ctx:
        keep = ctx.enter_context(tc.tile_pool(name="keep", bufs=1))
        flip_banks = ctx.enter_context(tc.psum_pool(name="flip_banks", bufs=2))
        product_banks = ctx.enter_context(tc.psum_pool(name="product_banks", bufs=PACK))
        weighted_banks = ctx.enter_context(tc.psum_pool(name="weighted_banks", bufs=2))
        banks = {"flip": flip_banks, "product": product_banks, "weighted": weighted_banks}

        def sbuf(shape, dtype, name):
            return keep.tile(shape, dtype, name=name, align_bytes=64)

        rows = {}
        feature_grouped, feature_codes, feature_scales = {}, {}, {}
        step_grouped, step_codes, step_scales = {}, {}, {}
        square_sums, inv_norms, inv_norm_rows = {}, {}, {}
        products, cosines, cos_grouped, cos_codes, cos_scales = {}, {}, {}, {}, {}
        cos_sums, inv_cos_sums = {}, {}

        def load(b, m, pieces):
            rows[m, b] = sbuf([P, MATRIX], BF16, "rows_%s%d" % (m, b))
            source = inputs[m][b].rearrange("(r t) h -> r (t h)", t=PACK)
            width = MATRIX // pieces
            for i in range(pieces):
                cols = slice(i * width, (i + 1) * width)
                nc.sync.dma_start(out=rows[m, b][:, cols], in_=source[:, cols])


        def regroup(engine, dst, src):
            if engine == "gpsimd":
                nc.gpsimd.tensor_scalar(
                    out=dst[:].rearrange("r (c t) -> r c t", t=PACK),
                    in0=src[:].rearrange("r (t c) -> r c t", t=PACK),
                    scalar1=1.0,
                    scalar2=0.0,
                    op0=ALU.mult,
                    op1=ALU.add,
                )
            else:
                copy = nc.vector.tensor_copy if engine == "vector" else nc.scalar.copy
                copy(
                    out=dst[:].rearrange("r (c i t) -> r c t i", i=4, t=PACK),
                    in_=src[:].rearrange("r (t c i) -> r c t i", i=4, t=PACK),
                )

        def quantise(grouped, name):
            codes = sbuf([P, MATRIX // PACK], U32, "codes_" + name)
            scales = sbuf([P, MATRIX // PACK], U8, "scales_" + name)
            nc.vector.quantize_mx(out=codes[:].bitcast(FP8X4), scales=scales[:], in_=grouped[:])
            return codes, scales

        def flip_features(b, m):
            words = rows[m, b][:].bitcast(F32)
            grouped = sbuf([P, MATRIX], BF16, "feature_grouped_%s%d" % (m, b))
            feature_grouped[m, b] = grouped
            grouped_words = grouped[:].bitcast(F32).rearrange("w (g t r u) -> w g t r u", g=2, t=2, u=2)
            for g in range(2):
                kind = ("flip", "weighted")[g]
                bank = banks[kind].tile([P, 2, 2, P], F32, name="flipped", tag=kind)
                for t in range(2):
                    for u in range(2):
                        first = (2 * g + t) * (FEATURES // 2) + u * P
                        nc.tensor.transpose(bank[:, t, u, :], words[:, first : first + P], identity[:])
                nc.vector.tensor_copy(out=grouped_words[:, g], in_=bank[:].rearrange("w t u r -> w t r u"))

        def quantise_features(b, m):
            feature_codes[m, b], feature_scales[m, b] = quantise(
                feature_grouped[m, b], "feature_%s%d" % (m, b)
            )

        def regroup_steps(engine, b, m):
            step_grouped[m, b] = sbuf([P, MATRIX], BF16, "step_grouped_%s%d" % (m, b))
            regroup(engine, step_grouped[m, b], rows[m, b])

        def quantise_steps(b, m):
            step_codes[m, b], step_scales[m, b] = quantise(step_grouped[m, b], "step_%s%d" % (m, b))


        def sum_squares(b, m):
            if b not in square_sums:
                square_sums[b] = sbuf([P, 2 * PACK], F32, "square_sums%d" % b)
            squares = sbuf([P, MATRIX], BF16, "squares_%s%d" % (m, b))
            for t in range(PACK):
                cols = slice(t * FEATURES, (t + 1) * FEATURES)
                nc.scalar.activation(
                    out=squares[:, cols],
                    in_=rows[m, b][:, cols],
                    func=ACT.Square,
                    accum_out=square_sums[b][:, FIRST[m] + t : FIRST[m] + t + 1],
                )

        def invert_norms(b):
            inv_squares = sbuf([P, 2 * PACK], F32, "inv_squares%d" % b)
            nc.vector.reciprocal(out=inv_squares[:], in_=square_sums[b][:])
            inv_norms[b] = sbuf([P, 2 * PACK], F32, "inv_norms%d" % b)
            nc.scalar.activation(out=inv_norms[b][:], in_=inv_squares[:], func=ACT.Sqrt)

        def spread_inv_norms(b, m):
            bank = flip_banks.tile([P, PACK, P], F32, name="spread", tag="flip")
            for t in range(PACK):
                column = inv_norms[b][:, FIRST[m] + t : FIRST[m] + t + 1]
                nc.tensor.matmul(
                    out=bank[:, t, :], lhsT=column.to_broadcast([P, P]), rhs=identity[:], start=True, stop=True
                )
            inv_norm_rows[m, b] = sbuf([P, STEPS], F32, "inv_norm_rows_%s%d" % (m, b))
            nc.scalar.copy(out=inv_norm_rows[m, b][:], in_=bank[:].rearrange("k t r -> k (t r)"))


        def multiply_features(b, m):
            o = OTHER[m]
            for t in range(PACK):
                tile_cols = slice(t * P, (t + 1) * P)
                products[m, b, t] = product_banks.tile([P, STEPS], F32, name="product", tag="product")
                nc.tensor.matmul_mx(
                    out=products[m, b, t][:],
                    lhsT=feature_codes[m, b][:, tile_cols].bitcast(FP8X4),
                    lhsT_scale=feature_scales[m, b][:, tile_cols],
                    rhs=feature_codes[o, b][:].bitcast(FP8X4),
                    rhs_scale=feature_scales[o, b][:],
                    start=True,
                    stop=True,
                )

        def normalise(b, m, t):
            if b not in cos_sums:
                cos_sums[b] = sbuf([P, 2 * PACK], F32, "cos_sums%d" % b)
            if (m, b) not in cosines:
                cosines[m, b] = sbuf([P, MATRIX], BF16, "cosines_%s%d" % (m, b))
            nc.vector.scalar_tensor_tensor(
                out=cosines[m, b][:, t * STEPS : (t + 1) * STEPS],
                in0=products[m, b, t][:],
                scalar=inv_norms[b][:, FIRST[m] + t : FIRST[m] + t + 1],
                in1=inv_norm_rows[OTHER[m], b][:],
                op0=ALU.mult,
                op1=ALU.mult,
                accum_out=cos_sums[b][:, FIRST[m] + t : FIRST[m] + t + 1],
            )

        def regroup_cosines(engine, b, m):
            cos_grouped[m, b] = sbuf([P, MATRIX], BF16, "cos_grouped_%s%d" % (m, b))
            regroup(engine, cos_grouped[m, b], cosines[m, b])

        def quantise_cosines(b, m):
            cos_codes[m, b], cos_scales[m, b] = quantise(cos_grouped[m, b], "cos_%s%d" % (m, b))

        def invert_cos_sums(b):
            inv_cos_sums[b] = sbuf([P, 2 * PACK], F32, "inv_cos_sums%d" % b)
            nc.vector.reciprocal(out=inv_cos_sums[b][:], in_=cos_sums[b][:])


        results = {}

        def mean_vectors(b, m, t, kind, engine):
            o = OTHER[m]
            if (m, b) not in results:
                results[m, b] = sbuf([P, PACK, FEATURES], F32, "result_%s%d" % (m, b))
            tile_cols = slice(t * P, (t + 1) * P)
            bank = banks[kind].tile([P, FEATURES], F32, name="weighted_sum", tag=kind)
            nc.tensor.matmul_mx(
                out=bank[:],
                lhsT=cos_codes[m, b][:, tile_cols].bitcast(FP8X4),
                lhsT_scale=cos_scales[m, b][:, tile_cols],
                rhs=step_codes[m, b][:].bitcast(FP8X4),
                rhs_scale=step_scales[m, b][:],
                start=True,
                stop=True,
            )
            inv_sum = inv_cos_sums[b][:, FIRST[o] + t : FIRST[o] + t + 1]
            if engine == "vector":
                nc.vector.tensor_scalar_mul(out=results[m, b][:, t, :], in0=bank[:], scalar1=inv_sum)
            else:
                nc.scalar.activation(out=results[m, b][:, t, :], in_=bank[:], func=ACT.Copy, scale=inv_sum)
            nc.sync.dma_start(
                out=outputs[m][b].rearrange("(r t) h -> r t h", t=PACK)[:, t, :], in_=results[m, b][:, t, :]
            )

        ctx.enter_context(tc.manual_schedule())

        identity = sbuf([P, P], F32, "identity")
        make_identity(nc, identity[:])
        one = sbuf([P, 1], F32, "one")
        nc.vector.memset(one[:], 1.0)
        warm = sbuf([P, 1], F32, "warm")
        nc.scalar.activation(out=warm[:], in_=one[:], func=ACT.Sqrt)

        for b in range(BATCH):
            for m in SIDES:
                load(b, m, pieces=2 if b == 0 else 1)

        for m in SIDES:
            regroup_steps("gpsimd", 0, m)
            sum_squares(0, m)
        for b in range(BATCH):
            for m in SIDES:
                flip_features(b, m)
        invert_norms(0)
        for b in range(BATCH):
            for m in SIDES:
                quantise_features(b, m)
        sum_squares(1, "p")
        spread_inv_norms(0, "q")
        multiply_features(0, "p")
        sum_squares(1, "q")
        spread_inv_norms(0, "p")
        for m in SIDES:
            quantise_steps(0, m)

        for t in range(PACK):
            normalise(0, "p", t)
        regroup_cosines("gpsimd", 0, "p")
        multiply_features(0, "q")
        invert_norms(1)
        regroup_steps("scalar", 1, "q")
        spread_inv_norms(1, "q")

        for t in range(PACK):
            normalise(0, "q", t)
        invert_cos_sums(0)
        regroup_cosines("gpsimd", 0, "q")
        multiply_features(1, "p")
        regroup_steps("scalar", 1, "p")
        spread_inv_norms(1, "p")
        quantise_steps(1, "q")
        quantise_cosines(0, "p")

        for t in range(PACK):
            normalise(1, "p", t)
            mean_vectors(0, "p", t, "weighted", "scalar")
        regroup_cosines("gpsimd", 1, "p")
        multiply_features(1, "q")
        quantise_steps(1, "p")
        quantise_cosines(0, "q")

        for t in range(PACK):
            normalise(1, "q", t)
            mean_vectors(0, "q", t, "weighted", "scalar")
        invert_cos_sums(1)
        quantise_cosines(1, "p")
        regroup_cosines("vector", 1, "q")

        for t in range(PACK):
            mean_vectors(1, "p", t, ("weighted", "product")[t % 2], "scalar")
        quantise_cosines(1, "q")
        for t in range(PACK):
            mean_vectors(1, "q", t, ("weighted", "product")[t % 2], ("vector", "scalar")[t % 2])
